import numpy as np
import ml_dtypes


def mxq(x, axis, fmt="e4m3"):
    dtype, down = {"e4m3": (ml_dtypes.float8_e4m3fn, 7), "e5m2": (ml_dtypes.float8_e5m2, 14)}[fmt]
    v = np.moveaxis(np.asarray(x, np.float32).astype(ml_dtypes.bfloat16).astype(np.float64), axis, -1)
    blocks = v.reshape(v.shape[:-1] + (-1, 32))
    amax = np.abs(blocks).max(-1, keepdims=True)
    byte = np.maximum(np.where(amax > 0, np.frexp(amax)[1] - 1 + 127, 0) - down, 1)
    scale = np.exp2(byte - 127.0)
    codes = (blocks / scale).astype(np.float32).astype(dtype).astype(np.float64)
    return np.moveaxis((codes * scale).reshape(v.shape), -1, axis)


WIDE = False


def mx_kscale(k):
    if not WIDE:
        return np.ones(k)
    levels = np.array([10, -10, 5, -5, 0])
    a = np.random.permutation(np.resize(levels, k // 512 * 4)).reshape(k // 512, 4)
    idx = np.arange(k)
    return np.exp2(a[idx // 512, idx % 128 // 32])


BF16 = ml_dtypes.bfloat16


def bf(x):
    return np.asarray(x, np.float32).astype(BF16)


def f64(x):
    return np.asarray(x).astype(np.float64)


E2M1 = np.array([0.0, 0.5, 1.0, 1.5, 2.0, 3.0, 4.0, 6.0, -0.0, -0.5, -1.0, -1.5, -2.0, -3.0, -4.0, -6.0])


def pack_weight(w, fmt):
    k, n = w.shape
    w = f64(bf(w)).reshape(k // 32, 32, n)
    amax = np.abs(w).max(1)
    if fmt == "e4m3":
        byte = np.frexp(amax)[1] - 1 + 127 - 7
    else:
        mant, ex = np.frexp(amax / 6.0)
        byte = np.where(mant > 0.5, ex, ex - 1) + 127
    byte = np.clip(np.where(amax > 0, byte, 1), 1, 254)
    scaled = (w * np.exp2(127.0 - byte)[:, None, :]).reshape(k, n).astype(np.float32)
    by_word = np.ascontiguousarray(scaled.reshape(k // 512, 128, 4, n).transpose(0, 1, 3, 2))
    if fmt == "e4m3":
        words = by_word.astype(ml_dtypes.float8_e4m3fn).view(np.uint8)
    else:
        c = by_word.astype(ml_dtypes.float4_e2m1fn).view(np.uint8) & 0xF
        words = c[..., 0::2] | (c[..., 1::2] << 4)
    return np.ascontiguousarray(words), np.ascontiguousarray(byte.astype(np.uint8).reshape(k // 512, 16, n))


def unpack_weight(words, scales, fmt):
    g, p, n, _ = words.shape
    if fmt == "e4m3":
        vals = np.ascontiguousarray(words).view(ml_dtypes.float8_e4m3fn).astype(np.float64)
    else:
        nib = np.empty((g, p, n, 4), np.uint8)
        nib[..., 0::2] = words & 0xF
        nib[..., 1::2] = words >> 4
        vals = E2M1[nib]
    vals = vals * np.repeat(np.exp2(scales.astype(np.float64) - 127.0), 8, axis=1)[..., None]
    return vals.transpose(0, 1, 3, 2).reshape(g * 512, n)


E, T, H, F = 4, 256, 1024, 512


def gelu_tanh(v):
    return 0.5 * v * (1.0 + np.tanh(np.sqrt(2.0 / np.pi) * (v + 0.044715 * v**3)))


def setup_inputs():
    s, t = mx_kscale(H), mx_kscale(F)
    w1 = np.random.standard_normal((E, H, 2 * F)) / np.sqrt(H) / s[:, None]
    w1[:, :, F:] *= t
    w2 = np.random.standard_normal((E, F, H)) * 1.5 / np.sqrt(F) / t[:, None]
    weight2_words, weight2_scales = pack_weight(w2.reshape(E * F, H), "e4m3")
    return {"x": bf(np.random.standard_normal((E, T, H)) * s),
            "weight1": bf(w1.reshape(H, E * 2 * F)),
            "weight2_words": weight2_words,
            "weight2_scales": weight2_scales}


def reference(x, weight1, weight2_words, weight2_scales):
    w1 = f64(weight1).reshape(E, H, 2 * F)
    w2 = unpack_weight(weight2_words, weight2_scales, "e4m3").reshape(E, F, H)
    h = mxq(f64(x), 2, "e4m3") @ mxq(w1, 1, "e4m3")
    a, b = h[..., :F], h[..., F:]
    g = gelu_tanh(a) * b
    return mxq(g, 2, "e4m3") @ w2

@@ -1,0 +1,202 @@
+from contextlib import ExitStack
+
+import concourse.mybir as mybir
+from concourse.masks import make_identity
+
+E, T, H, F = 4, 256, 1024, 512
+FLOPS = 2 * E * T * H * (2 * F) + 2 * E * T * F * H
+
+BF16 = mybir.dt.bfloat16
+F32 = mybir.dt.float32
+I32 = mybir.dt.int32
+U32 = mybir.dt.uint32
+U8 = mybir.dt.uint8
+FP8X4 = mybir.dt.float8_e4m3fn_x4
+
+P = 128
+PACK = 4
+K_PASS = P * PACK
+PASSES = H // K_PASS
+TOKEN_TILES = T // P
+HALVES = 2
+N_TILE = 512
+OUT_TILES = H // N_TILE
+
+VECTOR_Q = 84
+
+
+def tile_expert_kernel(tc, x, weight1, weight2_words, weight2_scales, out):
+    nc = tc.nc
+    with ExitStack() as stack:
+        pool = lambda name, bufs: stack.enter_context(tc.tile_pool(name=name, bufs=bufs))
+        bank = lambda name, bufs: stack.enter_context(tc.psum_pool(name=name, bufs=bufs))
+        consts = pool("consts", 1)
+        x_pool = pool("x_pool", E)
+        w1_pool = pool("w1_pool", E * PASSES)
+        w2_pool = pool("w2_pool", E)
+        out_pool = pool("out_pool", E)
+        x_work = pool("x_work", 2)
+        w1_group = pool("w1_group", 4)
+        w1_work = pool("w1_work", 2)
+        g_work = pool("g_work", 2)
+        xt_banks = bank("xt_banks", 2)
+        a_banks = bank("a_banks", 2)
+        b_banks = bank("b_banks", 2)
+        o_banks = bank("o_banks", 2)
+
+        w2_planes = consts.tile([P, H], U8, align_bytes=64)
+        nc.vector.memset(w2_planes[:].bitcast(I32), 0)
+        identity = consts.tile([P, P], F32)
+        make_identity(nc, identity[:])
+
+        x_rows, w1_rows, w2_bytes = [], [], []
+
+        def load_x(e):
+            rows = x_pool.tile([P, TOKEN_TILES, H], BF16, name="x_rows")
+            nc.sync.dma_start(out=rows[:], in_=x[e].rearrange("(p s) k -> p s k", s=TOKEN_TILES))
+            x_rows.append(rows)
+
+        def load_w1(e):
+            for c in range(PASSES):
+                rows = w1_pool.tile([P, PACK * 2 * F], BF16, name="w1_rows")
+                first = (e * PASSES + c) * P
+                nc.sync.dma_start(out=rows[:], in_=weight1[first : first + P, :])
+                w1_rows.append(rows)
+
+        def load_w2(e):
+            codes = w2_pool.tile([P, PACK * H], U8, name="w2_bytes", align_bytes=64)
+            nc.sync.dma_start(
+                out=codes[:].bitcast(I32),
+                in_=weight2_words[e].rearrange("p n t -> p (n t)").bitcast(I32),
+            )
+            w2_bytes.append(codes)
+
+        load_x(0)
+        load_w1(0)
+        load_x(1)
+        for quadrant in range(4):
+            nc.sync.dma_start(
+                out=w2_planes[32 * quadrant : 32 * quadrant + 4 * E, :].bitcast(I32),
+                in_=weight2_scales[:, 4 * quadrant : 4 * quadrant + 4, :].bitcast(I32),
+            )
+        load_w2(0)
+        for e in range(1, E):
+            load_w1(e)
+            if e + 1 < E:
+                load_x(e + 1)
+            load_w2(e)
+
+        def quantise_x(e):
+            grouped = x_work.tile([P, PASSES, T, PACK], BF16, name="x_grouped", align_bytes=64)
+            for c in range(PASSES):
+                xt = xt_banks.tile([P, 2, T], F32, name="xt")
+                for s in range(TOKEN_TILES):
+                    words = x_rows[e][:, s, c * K_PASS : (c + 1) * K_PASS].bitcast(F32)
+                    for u in range(2):
+                        nc.tensor.transpose(xt[:, u, s * P : (s + 1) * P], words[:, u::2], identity[:])
+                nc.scalar.copy(out=grouped[:, c].bitcast(F32), in_=xt[:].rearrange("p u k -> p k u"))
+            codes = x_work.tile([P, PASSES, T], U32, name="x_codes", align_bytes=64)
+            planes = x_work.tile([P, PASSES, T], U8, name="x_planes", align_bytes=64)
+            nc.vector.quantize_mx(
+                out=codes[:].rearrange("p c k -> p (c k)").bitcast(FP8X4),
+                scales=planes[:].rearrange("p c k -> p (c k)"),
+                in_=grouped[:].rearrange("p c k t -> p (c k t)"),
+            )
+            return codes, planes
+
+        def quantise_w1(e):
+            codes = w1_work.tile([P, PASSES, HALVES, F], U32, name="w1_codes", align_bytes=64)
+            planes = w1_work.tile([P, PASSES, HALVES, F], U8, name="w1_planes", align_bytes=64)
+            units = [(c, half) for c in range(PASSES) for half in range(HALVES)]
+            regrouped = []
+
+            def quantise_unit(i):
+                c, half = units[i]
+                nc.vector.quantize_mx(
+                    out=codes[:, c, half, :].bitcast(FP8X4),
+                    scales=planes[:, c, half, :],
+                    in_=regrouped[i][:].rearrange("p n t -> p (n t)"),
+                )
+
+            for i, (c, half) in enumerate(units):
+                rows = w1_rows[e * PASSES + c][:].rearrange(
+                    "p (t half q j) -> p half q t j", t=PACK, half=HALVES, j=PACK
+                )
+                grouped = w1_group.tile([P, F, PACK], BF16, name="w1_grouped", align_bytes=64)
+                sorted_view = grouped[:].rearrange("p (j q) t -> p q t j", j=PACK)
+                nc.vector.tensor_copy(out=sorted_view[:, :VECTOR_Q], in_=rows[:, half, :VECTOR_Q])
+                nc.scalar.copy(out=sorted_view[:, VECTOR_Q:], in_=rows[:, half, VECTOR_Q:])
+                regrouped.append(grouped)
+                if i > 0:
+                    quantise_unit(i - 1)
+            quantise_unit(len(units) - 1)
+            return codes, planes
+
+        def first_matmul(banks, half, s, x_q, w1_q):
+            x_codes, x_planes = x_q
+            w1_codes, w1_planes = w1_q
+            h_t = banks.tile([P, PACK, P], F32, name="h_t")
+            tokens = slice(s * P, (s + 1) * P)
+            for j in range(PACK):
+                columns = slice(j * P, (j + 1) * P)
+                for c in range(PASSES):
+                    nc.tensor.matmul_mx(
+                        out=h_t[:, j, :],
+                        lhsT=w1_codes[:, c, half, columns].bitcast(FP8X4),
+                        lhsT_scale=w1_planes[:, c, half, columns],
+                        rhs=x_codes[:, c, tokens].bitcast(FP8X4),
+                        rhs_scale=x_planes[:, c, tokens],
+                        start=(c == 0),
+                        stop=(c == PASSES - 1),
+                    )
+            return h_t
+
+        def expert(e, x_q):
+            w1_q = quantise_w1(e)
+            g_grouped = g_work.tile([P, TOKEN_TILES, P, PACK], BF16, name="g_grouped", align_bytes=64)
+            gelu_a = []
+            for s in range(TOKEN_TILES):
+                a_t = first_matmul(a_banks, 0, s, x_q, w1_q)
+                activated = g_work.tile([P, P, PACK], F32, name="activated")
+                nc.scalar.activation(
+                    out=activated[:],
+                    in_=a_t[:].rearrange("p j k -> p k j"),
+                    func=mybir.ActivationFunctionType.Gelu_apprx_tanh,
+                )
+                gelu_a.append(activated)
+            for s in range(TOKEN_TILES):
+                b_t = first_matmul(b_banks, 1, s, x_q, w1_q)
+                nc.vector.tensor_mul(
+                    out=g_grouped[:, s], in0=gelu_a[s][:], in1=b_t[:].rearrange("p j k -> p k j")
+                )
+            g_codes = g_work.tile([P, T], U32, name="g_codes", align_bytes=64)
+            g_planes = g_work.tile([P, T], U8, name="g_planes", align_bytes=64)
+            nc.vector.quantize_mx(
+                out=g_codes[:].bitcast(FP8X4),
+                scales=g_planes[:],
+                in_=g_grouped[:].rearrange("p s k t -> p (s k t)"),
+            )
+
+            result = out_pool.tile([P, TOKEN_TILES, H], F32, name="result")
+            out_rows = out[e].rearrange("(p s) n -> p s n", s=TOKEN_TILES)
+            for s in range(TOKEN_TILES):
+                tokens = slice(s * P, (s + 1) * P)
+                for n in range(OUT_TILES):
+                    o_ps = o_banks.tile([P, N_TILE], F32, name="o_ps")
+                    nc.tensor.matmul_mx(
+                        out=o_ps[:],
+                        lhsT=g_codes[:, tokens].bitcast(FP8X4),
+                        lhsT_scale=g_planes[:, tokens],
+                        rhs=w2_bytes[e][:, n * PACK * N_TILE : (n + 1) * PACK * N_TILE].bitcast(FP8X4),
+                        rhs_scale=w2_planes[4 * e : P, n * N_TILE : (n + 1) * N_TILE],
+                        start=True,
+                        stop=True,
+                    )
+                    nc.scalar.copy(out=result[:, s, n * N_TILE : (n + 1) * N_TILE], in_=o_ps[:])
+                nc.sync.dma_start(out=out_rows[:, s, :], in_=result[:, s, :])
+
+        x_q = quantise_x(0)
+        for e in range(E):
+            x_next = quantise_x(e + 1) if e + 1 < E else None
+            expert(e, x_q)
+            x_q = x_next

@@ -36,147 +36,137 @@ def tile_expert_kernel(tc, x, weight1, weight2_words, weight2_scales, out):
         w2_pool = pool("w2_pool", E)
         out_pool = pool("out_pool", E)
         x_work = pool("x_work", 2)
-        w1_group = pool("w1_group", 4)
+        w1_group = pool("w1_group", 3)
         w1_work = pool("w1_work", 2)
         g_work = pool("g_work", 2)
-        xt_banks = bank("xt_banks", 2)
-        a_banks = bank("a_banks", 2)
-        b_banks = bank("b_banks", 2)
+        xt_banks = bank("xt_banks", PASSES)
+        a_banks = bank("a_banks", TOKEN_TILES)
+        b_banks = bank("b_banks", TOKEN_TILES)
         o_banks = bank("o_banks", 2)
+        stack.enter_context(tc.manual_schedule())
 
         w2_planes = consts.tile([P, H], U8, align_bytes=64)
         nc.vector.memset(w2_planes[:].bitcast(I32), 0)
         identity = consts.tile([P, P], F32)
         make_identity(nc, identity[:])
 
-        x_rows, w1_rows, w2_bytes = [], [], []
-
-        def load_x(e):
-            rows = x_pool.tile([P, TOKEN_TILES, H], BF16, name="x_rows")
-            nc.sync.dma_start(out=rows[:], in_=x[e].rearrange("(p s) k -> p s k", s=TOKEN_TILES))
-            x_rows.append(rows)
-
-        def load_w1(e):
+        x_rows, w1_rows, w2_bytes = {}, {}, {}
+        for e in range(E):
             for c in range(PASSES):
-                rows = w1_pool.tile([P, PACK * 2 * F], BF16, name="w1_rows")
+                w1_rows[e, c] = w1_pool.tile([P, PACK * 2 * F], BF16, name="w1_rows")
                 first = (e * PASSES + c) * P
-                nc.sync.dma_start(out=rows[:], in_=weight1[first : first + P, :])
-                w1_rows.append(rows)
-
-        def load_w2(e):
-            codes = w2_pool.tile([P, PACK * H], U8, name="w2_bytes", align_bytes=64)
+                nc.sync.dma_start(out=w1_rows[e, c][:], in_=weight1[first : first + P, :])
+            x_rows[e] = x_pool.tile([P, TOKEN_TILES, H], BF16, name="x_rows")
+            nc.sync.dma_start(out=x_rows[e][:], in_=x[e].rearrange("(p s) k -> p s k", s=TOKEN_TILES))
+            if e == 0:
+                for quadrant in range(4):
+                    nc.sync.dma_start(
+                        out=w2_planes[32 * quadrant : 32 * quadrant + 4 * E, :].bitcast(I32),
+                        in_=weight2_scales[:, 4 * quadrant : 4 * quadrant + 4, :].bitcast(I32),
+                    )
+            w2_bytes[e] = w2_pool.tile([P, PACK * H], U8, name="w2_bytes", align_bytes=64)
             nc.sync.dma_start(
-                out=codes[:].bitcast(I32),
+                out=w2_bytes[e][:].bitcast(I32),
                 in_=weight2_words[e].rearrange("p n t -> p (n t)").bitcast(I32),
             )
-            w2_bytes.append(codes)
 
-        load_x(0)
-        load_w1(0)
-        load_x(1)
-        for quadrant in range(4):
-            nc.sync.dma_start(
-                out=w2_planes[32 * quadrant : 32 * quadrant + 4 * E, :].bitcast(I32),
-                in_=weight2_scales[:, 4 * quadrant : 4 * quadrant + 4, :].bitcast(I32),
-            )
-        load_w2(0)
-        for e in range(1, E):
-            load_w1(e)
-            if e + 1 < E:
-                load_x(e + 1)
-            load_w2(e)
+        units = [(c, half) for c in range(PASSES) for half in range(HALVES)]
+        x_bank, x_grouped, x_codes, x_planes = {}, {}, {}, {}
+        w1_grouped, w1_codes, w1_planes = {}, {}, {}
+        h_t, activated, g_grouped, g_codes, g_planes = {}, {}, {}, {}, {}
 
-        def quantise_x(e):
-            grouped = x_work.tile([P, PASSES, T, PACK], BF16, name="x_grouped", align_bytes=64)
+        def transpose_x(e):
             for c in range(PASSES):
-                xt = xt_banks.tile([P, 2, T], F32, name="xt")
+                x_bank[e, c] = xt_banks.tile([P, 2, T], F32, name="x_bank")
                 for s in range(TOKEN_TILES):
                     words = x_rows[e][:, s, c * K_PASS : (c + 1) * K_PASS].bitcast(F32)
                     for u in range(2):
-                        nc.tensor.transpose(xt[:, u, s * P : (s + 1) * P], words[:, u::2], identity[:])
-                nc.scalar.copy(out=grouped[:, c].bitcast(F32), in_=xt[:].rearrange("p u k -> p k u"))
-            codes = x_work.tile([P, PASSES, T], U32, name="x_codes", align_bytes=64)
-            planes = x_work.tile([P, PASSES, T], U8, name="x_planes", align_bytes=64)
+                        nc.tensor.transpose(
+                            x_bank[e, c][:, u, s * P : (s + 1) * P], words[:, u::2], identity[:]
+                        )
+
+        def regroup_x(e):
+            x_grouped[e] = x_work.tile([P, PASSES, T, PACK], BF16, name="x_grouped", align_bytes=64)
+            for c in range(PASSES):
+                nc.scalar.copy(
+                    out=x_grouped[e][:, c].bitcast(F32), in_=x_bank[e, c][:].rearrange("p u k -> p k u")
+                )
+
+        def quantise_x(e):
+            x_codes[e] = x_work.tile([P, PASSES, T], U32, name="x_codes", align_bytes=64)
+            x_planes[e] = x_work.tile([P, PASSES, T], U8, name="x_planes", align_bytes=64)
             nc.vector.quantize_mx(
-                out=codes[:].rearrange("p c k -> p (c k)").bitcast(FP8X4),
-                scales=planes[:].rearrange("p c k -> p (c k)"),
-                in_=grouped[:].rearrange("p c k t -> p (c k t)"),
+                out=x_codes[e][:].rearrange("p c k -> p (c k)").bitcast(FP8X4),
+                scales=x_planes[e][:].rearrange("p c k -> p (c k)"),
+                in_=x_grouped[e][:].rearrange("p c k t -> p (c k t)"),
             )
-            return codes, planes
 
-        def quantise_w1(e):
-            codes = w1_work.tile([P, PASSES, HALVES, F], U32, name="w1_codes", align_bytes=64)
-            planes = w1_work.tile([P, PASSES, HALVES, F], U8, name="w1_planes", align_bytes=64)
-            units = [(c, half) for c in range(PASSES) for half in range(HALVES)]
-            regrouped = []
+        def regroup_w1(e, i):
+            c, half = units[i]
+            rows = w1_rows[e, c][:].rearrange(
+                "p (t half q j) -> p half q t j", t=PACK, half=HALVES, j=PACK
+            )
+            w1_grouped[e, i] = w1_group.tile([P, F, PACK], BF16, name="w1_grouped", align_bytes=64)
+            sorted_view = w1_grouped[e, i][:].rearrange("p (j q) t -> p q t j", j=PACK)
+            nc.vector.tensor_copy(out=sorted_view[:, :VECTOR_Q], in_=rows[:, half, :VECTOR_Q])
+            nc.scalar.copy(out=sorted_view[:, VECTOR_Q:], in_=rows[:, half, VECTOR_Q:])
 
-            def quantise_unit(i):
-                c, half = units[i]
-                nc.vector.quantize_mx(
-                    out=codes[:, c, half, :].bitcast(FP8X4),
-                    scales=planes[:, c, half, :],
-                    in_=regrouped[i][:].rearrange("p n t -> p (n t)"),
-                )
+        def quantise_w1(e, i):
+            c, half = units[i]
+            if i == 0:
+                w1_codes[e] = w1_work.tile([P, PASSES, HALVES, F], U32, name="w1_codes", align_bytes=64)
+                w1_planes[e] = w1_work.tile([P, PASSES, HALVES, F], U8, name="w1_planes", align_bytes=64)
+            nc.vector.quantize_mx(
+                out=w1_codes[e][:, c, half, :].bitcast(FP8X4),
+                scales=w1_planes[e][:, c, half, :],
+                in_=w1_grouped[e, i][:].rearrange("p n t -> p (n t)"),
+            )
 
-            for i, (c, half) in enumerate(units):
-                rows = w1_rows[e * PASSES + c][:].rearrange(
-                    "p (t half q j) -> p half q t j", t=PACK, half=HALVES, j=PACK
-                )
-                grouped = w1_group.tile([P, F, PACK], BF16, name="w1_grouped", align_bytes=64)
-                sorted_view = grouped[:].rearrange("p (j q) t -> p q t j", j=PACK)
-                nc.vector.tensor_copy(out=sorted_view[:, :VECTOR_Q], in_=rows[:, half, :VECTOR_Q])
-                nc.scalar.copy(out=sorted_view[:, VECTOR_Q:], in_=rows[:, half, VECTOR_Q:])
-                regrouped.append(grouped)
-                if i > 0:
-                    quantise_unit(i - 1)
-            quantise_unit(len(units) - 1)
-            return codes, planes
-
-        def first_matmul(banks, half, s, x_q, w1_q):
-            x_codes, x_planes = x_q
-            w1_codes, w1_planes = w1_q
-            h_t = banks.tile([P, PACK, P], F32, name="h_t")
-            tokens = slice(s * P, (s + 1) * P)
-            for j in range(PACK):
-                columns = slice(j * P, (j + 1) * P)
-                for c in range(PASSES):
-                    nc.tensor.matmul_mx(
-                        out=h_t[:, j, :],
-                        lhsT=w1_codes[:, c, half, columns].bitcast(FP8X4),
-                        lhsT_scale=w1_planes[:, c, half, columns],
-                        rhs=x_codes[:, c, tokens].bitcast(FP8X4),
-                        rhs_scale=x_planes[:, c, tokens],
-                        start=(c == 0),
-                        stop=(c == PASSES - 1),
-                    )
-            return h_t
-
-        def expert(e, x_q):
-            w1_q = quantise_w1(e)
-            g_grouped = g_work.tile([P, TOKEN_TILES, P, PACK], BF16, name="g_grouped", align_bytes=64)
-            gelu_a = []
+        def first_matmul(e, half, banks):
             for s in range(TOKEN_TILES):
-                a_t = first_matmul(a_banks, 0, s, x_q, w1_q)
-                activated = g_work.tile([P, P, PACK], F32, name="activated")
+                h_t[e, half, s] = banks.tile([P, PACK, P], F32, name="h_t")
+                tokens = slice(s * P, (s + 1) * P)
+                for j in range(PACK):
+                    columns = slice(j * P, (j + 1) * P)
+                    for c in range(PASSES):
+                        nc.tensor.matmul_mx(
+                            out=h_t[e, half, s][:, j, :],
+                            lhsT=w1_codes[e][:, c, half, columns].bitcast(FP8X4),
+                            lhsT_scale=w1_planes[e][:, c, half, columns],
+                            rhs=x_codes[e][:, c, tokens].bitcast(FP8X4),
+                            rhs_scale=x_planes[e][:, c, tokens],
+                            start=(c == 0),
+                            stop=(c == PASSES - 1),
+                        )
+
+        def gelu(e):
+            for s in range(TOKEN_TILES):
+                activated[e, s] = g_work.tile([P, P, PACK], F32, name="activated")
                 nc.scalar.activation(
-                    out=activated[:],
-                    in_=a_t[:].rearrange("p j k -> p k j"),
+                    out=activated[e, s][:],
+                    in_=h_t[e, 0, s][:].rearrange("p j k -> p k j"),
                     func=mybir.ActivationFunctionType.Gelu_apprx_tanh,
                 )
-                gelu_a.append(activated)
+
+        def gate(e):
+            g_grouped[e] = g_work.tile([P, TOKEN_TILES, P, PACK], BF16, name="g_grouped", align_bytes=64)
             for s in range(TOKEN_TILES):
-                b_t = first_matmul(b_banks, 1, s, x_q, w1_q)
                 nc.vector.tensor_mul(
-                    out=g_grouped[:, s], in0=gelu_a[s][:], in1=b_t[:].rearrange("p j k -> p k j")
+                    out=g_grouped[e][:, s],
+                    in0=activated[e, s][:],
+                    in1=h_t[e, 1, s][:].rearrange("p j k -> p k j"),
                 )
-            g_codes = g_work.tile([P, T], U32, name="g_codes", align_bytes=64)
-            g_planes = g_work.tile([P, T], U8, name="g_planes", align_bytes=64)
+
+        def quantise_g(e):
+            g_codes[e] = g_work.tile([P, T], U32, name="g_codes", align_bytes=64)
+            g_planes[e] = g_work.tile([P, T], U8, name="g_planes", align_bytes=64)
             nc.vector.quantize_mx(
-                out=g_codes[:].bitcast(FP8X4),
-                scales=g_planes[:],
-                in_=g_grouped[:].rearrange("p s k t -> p (s k t)"),
+                out=g_codes[e][:].bitcast(FP8X4),
+                scales=g_planes[e][:],
+                in_=g_grouped[e][:].rearrange("p s k t -> p (s k t)"),
             )
 
+        def second_matmul(e):
             result = out_pool.tile([P, TOKEN_TILES, H], F32, name="result")
             out_rows = out[e].rearrange("(p s) n -> p s n", s=TOKEN_TILES)
             for s in range(TOKEN_TILES):
@@ -185,8 +175,8 @@ def tile_expert_kernel(tc, x, weight1, weight2_words, weight2_scales, out):
                     o_ps = o_banks.tile([P, N_TILE], F32, name="o_ps")
                     nc.tensor.matmul_mx(
                         out=o_ps[:],
-                        lhsT=g_codes[:, tokens].bitcast(FP8X4),
-                        lhsT_scale=g_planes[:, tokens],
+                        lhsT=g_codes[e][:, tokens].bitcast(FP8X4),
+                        lhsT_scale=g_planes[e][:, tokens],
                         rhs=w2_bytes[e][:, n * PACK * N_TILE : (n + 1) * PACK * N_TILE].bitcast(FP8X4),
                         rhs_scale=w2_planes[4 * e : P, n * N_TILE : (n + 1) * N_TILE],
                         start=True,
@@ -195,8 +185,32 @@ def tile_expert_kernel(tc, x, weight1, weight2_words, weight2_scales, out):
                     nc.scalar.copy(out=result[:, s, n * N_TILE : (n + 1) * N_TILE], in_=o_ps[:])
                 nc.sync.dma_start(out=out_rows[:, s, :], in_=result[:, s, :])
 
-        x_q = quantise_x(0)
-        for e in range(E):
-            x_next = quantise_x(e + 1) if e + 1 < E else None
-            expert(e, x_q)
-            x_q = x_next
+        for e in range(E + 1):
+            this = e < E
+            last = e > 0
+            if this:
+                regroup_w1(e, 0)
+            if last:
+                quantise_w1(e - 1, 3)
+                gelu(e - 1)
+                first_matmul(e - 1, 1, b_banks)
+            if this:
+                regroup_w1(e, 1)
+                quantise_w1(e, 0)
+            if last:
+                gate(e - 1)
+            if this:
+                transpose_x(e)
+                regroup_w1(e, 2)
+            if last:
+                quantise_g(e - 1)
+            if this:
+                quantise_w1(e, 1)
+                regroup_x(e)
+                regroup_w1(e, 3)
+                quantise_w1(e, 2)
+                quantise_x(e)
+            if last:
+                second_matmul(e - 1)
+            if this:
+                first_matmul(e, 0, a_banks)

@@ -22,7 +22,7 @@ HALVES = 2
 N_TILE = 512
 OUT_TILES = H // N_TILE
 
-VECTOR_Q = 84
+VECTOR_Q = 88
 
 
 def tile_expert_kernel(tc, x, weight1, weight2_words, weight2_scales, out):
@@ -51,29 +51,43 @@ def tile_expert_kernel(tc, x, weight1, weight2_words, weight2_scales, out):
         make_identity(nc, identity[:])
 
         x_rows, w1_rows, w2_bytes = {}, {}, {}
-        for e in range(E):
+
+        def load_x(e):
+            x_rows[e] = x_pool.tile([P, TOKEN_TILES, H], BF16, name="x_rows")
+            nc.sync.dma_start(out=x_rows[e][:], in_=x[e].rearrange("(p s) k -> p s k", s=TOKEN_TILES))
+
+        def load_w1(e):
             for c in range(PASSES):
                 w1_rows[e, c] = w1_pool.tile([P, PACK * 2 * F], BF16, name="w1_rows")
                 first = (e * PASSES + c) * P
                 nc.sync.dma_start(out=w1_rows[e, c][:], in_=weight1[first : first + P, :])
-            x_rows[e] = x_pool.tile([P, TOKEN_TILES, H], BF16, name="x_rows")
-            nc.sync.dma_start(out=x_rows[e][:], in_=x[e].rearrange("(p s) k -> p s k", s=TOKEN_TILES))
-            if e == 0:
-                for quadrant in range(4):
-                    nc.sync.dma_start(
-                        out=w2_planes[32 * quadrant : 32 * quadrant + 4 * E, :].bitcast(I32),
-                        in_=weight2_scales[:, 4 * quadrant : 4 * quadrant + 4, :].bitcast(I32),
-                    )
+
+        def load_w2(e):
             w2_bytes[e] = w2_pool.tile([P, PACK * H], U8, name="w2_bytes", align_bytes=64)
             nc.sync.dma_start(
                 out=w2_bytes[e][:].bitcast(I32),
                 in_=weight2_words[e].rearrange("p n t -> p (n t)").bitcast(I32),
             )
 
+        load_x(0)
+        for e in range(E):
+            load_w1(e)
+            if e + 1 < E:
+                load_x(e + 1)
+            if e == 1:
+                for quadrant in range(4):
+                    nc.sync.dma_start(
+                        out=w2_planes[32 * quadrant : 32 * quadrant + 4 * E, :].bitcast(I32),
+                        in_=weight2_scales[:, 4 * quadrant : 4 * quadrant + 4, :].bitcast(I32),
+                    )
+            if e > 0:
+                load_w2(e - 1)
+        load_w2(E - 1)
+
         units = [(c, half) for c in range(PASSES) for half in range(HALVES)]
         x_bank, x_grouped, x_codes, x_planes = {}, {}, {}, {}
         w1_grouped, w1_codes, w1_planes = {}, {}, {}
-        h_t, activated, g_grouped, g_codes, g_planes = {}, {}, {}, {}, {}
+        h_t, activated, g_grouped, g_codes, g_planes, result = {}, {}, {}, {}, {}, {}
 
         def transpose_x(e):
             for c in range(PASSES):
@@ -148,69 +162,88 @@ def tile_expert_kernel(tc, x, weight1, weight2_words, weight2_scales, out):
                     func=mybir.ActivationFunctionType.Gelu_apprx_tanh,
                 )
 
-        def gate(e):
-            g_grouped[e] = g_work.tile([P, TOKEN_TILES, P, PACK], BF16, name="g_grouped", align_bytes=64)
-            for s in range(TOKEN_TILES):
-                nc.vector.tensor_mul(
-                    out=g_grouped[e][:, s],
-                    in0=activated[e, s][:],
-                    in1=h_t[e, 1, s][:].rearrange("p j k -> p k j"),
+        def gate(e, s):
+            if s == 0:
+                g_grouped[e] = g_work.tile(
+                    [P, TOKEN_TILES, P, PACK], BF16, name="g_grouped", align_bytes=64
                 )
-
-        def quantise_g(e):
-            g_codes[e] = g_work.tile([P, T], U32, name="g_codes", align_bytes=64)
-            g_planes[e] = g_work.tile([P, T], U8, name="g_planes", align_bytes=64)
-            nc.vector.quantize_mx(
-                out=g_codes[e][:].bitcast(FP8X4),
-                scales=g_planes[e][:],
-                in_=g_grouped[e][:].rearrange("p s k t -> p (s k t)"),
+            nc.vector.tensor_mul(
+                out=g_grouped[e][:, s],
+                in0=activated[e, s][:],
+                in1=h_t[e, 1, s][:].rearrange("p j k -> p k j"),
             )
 
-        def second_matmul(e):
-            result = out_pool.tile([P, TOKEN_TILES, H], F32, name="result")
-            out_rows = out[e].rearrange("(p s) n -> p s n", s=TOKEN_TILES)
-            for s in range(TOKEN_TILES):
-                tokens = slice(s * P, (s + 1) * P)
-                for n in range(OUT_TILES):
-                    o_ps = o_banks.tile([P, N_TILE], F32, name="o_ps")
-                    nc.tensor.matmul_mx(
-                        out=o_ps[:],
-                        lhsT=g_codes[e][:, tokens].bitcast(FP8X4),
-                        lhsT_scale=g_planes[e][:, tokens],
-                        rhs=w2_bytes[e][:, n * PACK * N_TILE : (n + 1) * PACK * N_TILE].bitcast(FP8X4),
-                        rhs_scale=w2_planes[4 * e : P, n * N_TILE : (n + 1) * N_TILE],
-                        start=True,
-                        stop=True,
-                    )
-                    nc.scalar.copy(out=result[:, s, n * N_TILE : (n + 1) * N_TILE], in_=o_ps[:])
-                nc.sync.dma_start(out=out_rows[:, s, :], in_=result[:, s, :])
+        def quantise_g(e, s):
+            if s == 0:
+                g_codes[e] = g_work.tile([P, T], U32, name="g_codes", align_bytes=64)
+                g_planes[e] = g_work.tile([P, T], U8, name="g_planes", align_bytes=64)
+            tokens = slice(s * P, (s + 1) * P)
+            nc.vector.quantize_mx(
+                out=g_codes[e][:, tokens].bitcast(FP8X4),
+                scales=g_planes[e][:, tokens],
+                in_=g_grouped[e][:, s].rearrange("p k t -> p (k t)"),
+            )
 
+        def second_matmul(e, s, odd_bank_copy):
+            if s == 0:
+                result[e] = out_pool.tile([P, TOKEN_TILES, H], F32, name="result")
+            tokens = slice(s * P, (s + 1) * P)
+            for n in range(OUT_TILES):
+                o_ps = o_banks.tile([P, N_TILE], F32, name="o_ps")
+                nc.tensor.matmul_mx(
+                    out=o_ps[:],
+                    lhsT=g_codes[e][:, tokens].bitcast(FP8X4),
+                    lhsT_scale=g_planes[e][:, tokens],
+                    rhs=w2_bytes[e][:, n * PACK * N_TILE : (n + 1) * PACK * N_TILE].bitcast(FP8X4),
+                    rhs_scale=w2_planes[4 * e : P, n * N_TILE : (n + 1) * N_TILE],
+                    start=True,
+                    stop=True,
+                )
+                copy = odd_bank_copy if n % 2 else nc.scalar.copy
+                copy(out=result[e][:, s, n * N_TILE : (n + 1) * N_TILE], in_=o_ps[:])
+            out_rows = out[e].rearrange("(p s) n -> p s n", s=TOKEN_TILES)
+            nc.sync.dma_start(out=out_rows[:, s, :], in_=result[e][:, s, :])
+
+        transpose_x(0)
+        regroup_x(0)
+        quantise_x(0)
         for e in range(E + 1):
             this = e < E
             last = e > 0
+            ahead = e + 1 < E
+            odd_bank_copy = nc.scalar.copy if this else nc.vector.tensor_copy
             if this:
                 regroup_w1(e, 0)
             if last:
                 quantise_w1(e - 1, 3)
-                gelu(e - 1)
                 first_matmul(e - 1, 1, b_banks)
+                gelu(e - 1)
             if this:
                 regroup_w1(e, 1)
                 quantise_w1(e, 0)
             if last:
-                gate(e - 1)
+                gate(e - 1, 0)
+            if ahead:
+                transpose_x(e + 1)
             if this:
-                transpose_x(e)
                 regroup_w1(e, 2)
             if last:
-                quantise_g(e - 1)
+                quantise_g(e - 1, 0)
+                gate(e - 1, 1)
             if this:
                 quantise_w1(e, 1)
-                regroup_x(e)
+            if last:
+                quantise_g(e - 1, 1)
+            if ahead:
+                regroup_x(e + 1)
+            if last:
+                second_matmul(e - 1, 0, odd_bank_copy)
+            if this:
                 regroup_w1(e, 3)
                 quantise_w1(e, 2)
-                quantise_x(e)
+            if ahead:
+                quantise_x(e + 1)
             if last:
-                second_matmul(e - 1)
+                second_matmul(e - 1, 1, odd_bank_copy)
             if this:
                 first_matmul(e, 0, a_banks)

@@ -22,7 +22,7 @@ HALVES = 2
 N_TILE = 512
 OUT_TILES = H // N_TILE
 
-VECTOR_Q = 88
+VECTOR_Q = 84
 
 
 def tile_expert_kernel(tc, x, weight1, weight2_words, weight2_scales, out):
@@ -41,14 +41,19 @@ def tile_expert_kernel(tc, x, weight1, weight2_words, weight2_scales, out):
         g_work = pool("g_work", 2)
         xt_banks = bank("xt_banks", PASSES)
         a_banks = bank("a_banks", TOKEN_TILES)
-        b_banks = bank("b_banks", TOKEN_TILES)
-        o_banks = bank("o_banks", 2)
+        bo_banks = bank("bo_banks", 4)
         stack.enter_context(tc.manual_schedule())
 
         w2_planes = consts.tile([P, H], U8, align_bytes=64)
         nc.vector.memset(w2_planes[:].bitcast(I32), 0)
         identity = consts.tile([P, P], F32)
         make_identity(nc, identity[:])
+        table_warmer = consts.tile([P, 1], F32)
+        nc.scalar.activation(
+            out=table_warmer[:],
+            in_=identity[:, 0:1],
+            func=mybir.ActivationFunctionType.Gelu_apprx_tanh,
+        )
 
         x_rows, w1_rows, w2_bytes = {}, {}, {}
 
@@ -136,9 +141,9 @@ def tile_expert_kernel(tc, x, weight1, weight2_words, weight2_scales, out):
                 in_=w1_grouped[e, i][:].rearrange("p n t -> p (n t)"),
             )
 
-        def first_matmul(e, half, banks):
+        def first_matmul(e, half, banks, tag):
             for s in range(TOKEN_TILES):
-                h_t[e, half, s] = banks.tile([P, PACK, P], F32, name="h_t")
+                h_t[e, half, s] = banks.tile([P, PACK, P], F32, name="h_t", tag=tag)
                 tokens = slice(s * P, (s + 1) * P)
                 for j in range(PACK):
                     columns = slice(j * P, (j + 1) * P)
@@ -188,8 +193,9 @@ def tile_expert_kernel(tc, x, weight1, weight2_words, weight2_scales, out):
             if s == 0:
                 result[e] = out_pool.tile([P, TOKEN_TILES, H], F32, name="result")
             tokens = slice(s * P, (s + 1) * P)
+            out_rows = out[e].rearrange("(p s) n -> p s n", s=TOKEN_TILES)
             for n in range(OUT_TILES):
-                o_ps = o_banks.tile([P, N_TILE], F32, name="o_ps")
+                o_ps = bo_banks.tile([P, N_TILE], F32, name="o_ps", tag="bo")
                 nc.tensor.matmul_mx(
                     out=o_ps[:],
                     lhsT=g_codes[e][:, tokens].bitcast(FP8X4),
@@ -200,13 +206,12 @@ def tile_expert_kernel(tc, x, weight1, weight2_words, weight2_scales, out):
                     stop=True,
                 )
                 copy = odd_bank_copy if n % 2 else nc.scalar.copy
-                copy(out=result[e][:, s, n * N_TILE : (n + 1) * N_TILE], in_=o_ps[:])
-            out_rows = out[e].rearrange("(p s) n -> p s n", s=TOKEN_TILES)
-            nc.sync.dma_start(out=out_rows[:, s, :], in_=result[e][:, s, :])
+                columns = slice(n * N_TILE, (n + 1) * N_TILE)
+                copy(out=result[e][:, s, columns], in_=o_ps[:])
+                nc.sync.dma_start(out=out_rows[:, s, columns], in_=result[e][:, s, columns])
 
         transpose_x(0)
         regroup_x(0)
-        quantise_x(0)
         for e in range(E + 1):
             this = e < E
             last = e > 0
@@ -214,9 +219,10 @@ def tile_expert_kernel(tc, x, weight1, weight2_words, weight2_scales, out):
             odd_bank_copy = nc.scalar.copy if this else nc.vector.tensor_copy
             if this:
                 regroup_w1(e, 0)
+                quantise_x(e)
             if last:
                 quantise_w1(e - 1, 3)
-                first_matmul(e - 1, 1, b_banks)
+                first_matmul(e - 1, 1, bo_banks, "bo")
                 gelu(e - 1)
             if this:
                 regroup_w1(e, 1)
@@ -234,16 +240,15 @@ def tile_expert_kernel(tc, x, weight1, weight2_words, weight2_scales, out):
                 quantise_w1(e, 1)
             if last:
                 quantise_g(e - 1, 1)
+            if this:
+                quantise_w1(e, 2)
             if ahead:
                 regroup_x(e + 1)
             if last:
                 second_matmul(e - 1, 0, odd_bank_copy)
             if this:
                 regroup_w1(e, 3)
-                quantise_w1(e, 2)
-            if ahead:
-                quantise_x(e + 1)
             if last:
                 second_matmul(e - 1, 1, odd_bank_copy)
             if this:
-                first_matmul(e, 0, a_banks)
+                first_matmul(e, 0, a_banks, "a")

@@ -32,7 +32,8 @@ def tile_expert_kernel(tc, x, weight1, weight2_words, weight2_scales, out):
         bank = lambda name, bufs: stack.enter_context(tc.psum_pool(name=name, bufs=bufs))
         consts = pool("consts", 1)
         x_pool = pool("x_pool", E)
-        w1_pool = pool("w1_pool", E * PASSES)
+        w1_pool = pool("w1_pool", (E - 1) * PASSES)
+        w1_first = pool("w1_first", PASSES * HALVES)
         w2_pool = pool("w2_pool", E)
         out_pool = pool("out_pool", E)
         x_work = pool("x_work", 2)
@@ -61,11 +62,20 @@ def tile_expert_kernel(tc, x, weight1, weight2_words, weight2_scales, out):
             x_rows[e] = x_pool.tile([P, TOKEN_TILES, H], BF16, name="x_rows")
             nc.sync.dma_start(out=x_rows[e][:], in_=x[e].rearrange("(p s) k -> p s k", s=TOKEN_TILES))
 
-        def load_w1(e):
-            for c in range(PASSES):
-                w1_rows[e, c] = w1_pool.tile([P, PACK * 2 * F], BF16, name="w1_rows")
-                first = (e * PASSES + c) * P
-                nc.sync.dma_start(out=w1_rows[e, c][:], in_=weight1[first : first + P, :])
+        def load_w1(e, c):
+            first = (e * PASSES + c) * P
+            tile_rows = w1_pool.tile([P, PACK * 2 * F], BF16, name="w1_rows")
+            nc.sync.dma_start(out=tile_rows[:], in_=weight1[first : first + P, :])
+            view = tile_rows[:].rearrange("p (t half q j) -> p half q t j", t=PACK, half=HALVES, j=PACK)
+            for half in range(HALVES):
+                w1_rows[e, c, half] = view[:, half]
+
+        def load_w1_quarter(e, c, half):
+            first = (e * PASSES + c) * P
+            tile_rows = w1_first.tile([P, PACK, F], BF16, name="w1_quarter")
+            source = weight1[first : first + P, :].rearrange("p (t half n) -> p half t n", t=PACK, half=HALVES)
+            nc.sync.dma_start(out=tile_rows[:], in_=source[:, half])
+            w1_rows[e, c, half] = tile_rows[:].rearrange("p t (q j) -> p q t j", j=PACK)
 
         def load_w2(e):
             w2_bytes[e] = w2_pool.tile([P, PACK * H], U8, name="w2_bytes", align_bytes=64)
@@ -74,19 +84,22 @@ def tile_expert_kernel(tc, x, weight1, weight2_words, weight2_scales, out):
                 in_=weight2_words[e].rearrange("p n t -> p (n t)").bitcast(I32),
             )
 
+        load_w1_quarter(0, 0, 0)
+        load_w1_quarter(0, 0, 1)
         load_x(0)
-        for e in range(E):
-            load_w1(e)
-            if e + 1 < E:
-                load_x(e + 1)
+        load_w1_quarter(0, 1, 0)
+        load_w1_quarter(0, 1, 1)
+        for e in range(1, E):
+            load_w1(e, 0)
+            load_x(e)
+            load_w1(e, 1)
             if e == 1:
                 for quadrant in range(4):
                     nc.sync.dma_start(
                         out=w2_planes[32 * quadrant : 32 * quadrant + 4 * E, :].bitcast(I32),
                         in_=weight2_scales[:, 4 * quadrant : 4 * quadrant + 4, :].bitcast(I32),
                     )
-            if e > 0:
-                load_w2(e - 1)
+            load_w2(e - 1)
         load_w2(E - 1)
 
         units = [(c, half) for c in range(PASSES) for half in range(HALVES)]
@@ -122,13 +135,11 @@ def tile_expert_kernel(tc, x, weight1, weight2_words, weight2_scales, out):
 
         def regroup_w1(e, i):
             c, half = units[i]
-            rows = w1_rows[e, c][:].rearrange(
-                "p (t half q j) -> p half q t j", t=PACK, half=HALVES, j=PACK
-            )
+            rows = w1_rows[e, c, half]
             w1_grouped[e, i] = w1_group.tile([P, F, PACK], BF16, name="w1_grouped", align_bytes=64)
             sorted_view = w1_grouped[e, i][:].rearrange("p (j q) t -> p q t j", j=PACK)
-            nc.vector.tensor_copy(out=sorted_view[:, :VECTOR_Q], in_=rows[:, half, :VECTOR_Q])
-            nc.scalar.copy(out=sorted_view[:, VECTOR_Q:], in_=rows[:, half, VECTOR_Q:])
+            nc.vector.tensor_copy(out=sorted_view[:, :VECTOR_Q], in_=rows[:, :VECTOR_Q])
+            nc.scalar.copy(out=sorted_view[:, VECTOR_Q:], in_=rows[:, VECTOR_Q:])
 
         def quantise_w1(e, i):
             c, half = units[i]
@@ -210,16 +221,12 @@ def tile_expert_kernel(tc, x, weight1, weight2_words, weight2_scales, out):
                 copy(out=result[e][:, s, columns], in_=o_ps[:])
                 nc.sync.dma_start(out=out_rows[:, s, columns], in_=result[e][:, s, columns])
 
-        transpose_x(0)
-        regroup_x(0)
         for e in range(E + 1):
             this = e < E
             last = e > 0
-            ahead = e + 1 < E
             odd_bank_copy = nc.scalar.copy if this else nc.vector.tensor_copy
             if this:
                 regroup_w1(e, 0)
-                quantise_x(e)
             if last:
                 quantise_w1(e - 1, 3)
                 first_matmul(e - 1, 1, bo_banks, "bo")
@@ -229,9 +236,8 @@ def tile_expert_kernel(tc, x, weight1, weight2_words, weight2_scales, out):
                 quantise_w1(e, 0)
             if last:
                 gate(e - 1, 0)
-            if ahead:
-                transpose_x(e + 1)
             if this:
+                transpose_x(e)
                 regroup_w1(e, 2)
             if last:
                 quantise_g(e - 1, 0)
@@ -241,9 +247,9 @@ def tile_expert_kernel(tc, x, weight1, weight2_words, weight2_scales, out):
             if last:
                 quantise_g(e - 1, 1)
             if this:
+                regroup_x(e)
                 quantise_w1(e, 2)
-            if ahead:
-                regroup_x(e + 1)
+                quantise_x(e)
             if last:
                 second_matmul(e - 1, 0, odd_bank_copy)
             if this:

@@ -32,8 +32,7 @@ def tile_expert_kernel(tc, x, weight1, weight2_words, weight2_scales, out):
         bank = lambda name, bufs: stack.enter_context(tc.psum_pool(name=name, bufs=bufs))
         consts = pool("consts", 1)
         x_pool = pool("x_pool", E)
-        w1_pool = pool("w1_pool", (E - 1) * PASSES)
-        w1_first = pool("w1_first", PASSES * HALVES)
+        w1_pool = pool("w1_pool", E * PASSES)
         w2_pool = pool("w2_pool", E)
         out_pool = pool("out_pool", E)
         x_work = pool("x_work", 2)
@@ -70,12 +69,6 @@ def tile_expert_kernel(tc, x, weight1, weight2_words, weight2_scales, out):
             for half in range(HALVES):
                 w1_rows[e, c, half] = view[:, half]
 
-        def load_w1_quarter(e, c, half):
-            first = (e * PASSES + c) * P
-            tile_rows = w1_first.tile([P, PACK, F], BF16, name="w1_quarter")
-            source = weight1[first : first + P, :].rearrange("p (t half n) -> p half t n", t=PACK, half=HALVES)
-            nc.sync.dma_start(out=tile_rows[:], in_=source[:, half])
-            w1_rows[e, c, half] = tile_rows[:].rearrange("p t (q j) -> p q t j", j=PACK)
 
         def load_w2(e):
             w2_bytes[e] = w2_pool.tile([P, PACK * H], U8, name="w2_bytes", align_bytes=64)
@@ -84,12 +77,7 @@ def tile_expert_kernel(tc, x, weight1, weight2_words, weight2_scales, out):
                 in_=weight2_words[e].rearrange("p n t -> p (n t)").bitcast(I32),
             )
 
-        load_w1_quarter(0, 0, 0)
-        load_w1_quarter(0, 0, 1)
-        load_x(0)
-        load_w1_quarter(0, 1, 0)
-        load_w1_quarter(0, 1, 1)
-        for e in range(1, E):
+        for e in range(E):
             load_w1(e, 0)
             load_x(e)
             load_w1(e, 1)
@@ -99,7 +87,8 @@ def tile_expert_kernel(tc, x, weight1, weight2_words, weight2_scales, out):
                         out=w2_planes[32 * quadrant : 32 * quadrant + 4 * E, :].bitcast(I32),
                         in_=weight2_scales[:, 4 * quadrant : 4 * quadrant + 4, :].bitcast(I32),
                     )
-            load_w2(e - 1)
+            if e > 0:
+                load_w2(e - 1)
         load_w2(E - 1)
 
         units = [(c, half) for c in range(PASSES) for half in range(HALVES)]
@@ -221,7 +210,18 @@ def tile_expert_kernel(tc, x, weight1, weight2_words, weight2_scales, out):
                 copy(out=result[e][:, s, columns], in_=o_ps[:])
                 nc.sync.dma_start(out=out_rows[:, s, columns], in_=result[e][:, s, columns])
 
-        for e in range(E + 1):
+        regroup_w1(0, 0)
+        regroup_w1(0, 1)
+        quantise_w1(0, 0)
+        transpose_x(0)
+        quantise_w1(0, 1)
+        regroup_x(0)
+        regroup_w1(0, 2)
+        quantise_x(0)
+        quantise_w1(0, 2)
+        regroup_w1(0, 3)
+        first_matmul(0, 0, a_banks, "a")
+        for e in range(1, E + 1):
             this = e < E
             last = e > 0
             odd_bank_copy = nc.scalar.copy if this else nc.vector.tensor_copy

@@ -22,7 +22,7 @@ HALVES = 2
 N_TILE = 512
 OUT_TILES = H // N_TILE
 
-VECTOR_Q = 84
+VECTOR_Q = 80
 
 
 def tile_expert_kernel(tc, x, weight1, weight2_words, weight2_scales, out):

@@ -91,10 +91,14 @@ def tile_expert_kernel(tc, x, weight1, weight2_words, weight2_scales, out):
                 load_w2(e - 1)
         load_w2(E - 1)
 
-        units = [(c, half) for c in range(PASSES) for half in range(HALVES)]
+        def units(e):
+            if e < E - 1:
+                return [(c, half) for c in range(PASSES) for half in range(HALVES)]
+            return [(c, half) for half in range(HALVES) for c in range(PASSES)]
+
         x_bank, x_grouped, x_codes, x_planes = {}, {}, {}, {}
         w1_grouped, w1_codes, w1_planes = {}, {}, {}
-        h_t, activated, g_grouped, g_codes, g_planes, result = {}, {}, {}, {}, {}, {}
+        h_t, activated, g_grouped, g_codes, g_planes, out_bank, result = {}, {}, {}, {}, {}, {}, {}
 
         def transpose_x(e):
             for c in range(PASSES):
@@ -123,7 +127,7 @@ def tile_expert_kernel(tc, x, weight1, weight2_words, weight2_scales, out):
             )
 
         def regroup_w1(e, i):
-            c, half = units[i]
+            c, half = units(e)[i]
             rows = w1_rows[e, c, half]
             w1_grouped[e, i] = w1_group.tile([P, F, PACK], BF16, name="w1_grouped", align_bytes=64)
             sorted_view = w1_grouped[e, i][:].rearrange("p (j q) t -> p q t j", j=PACK)
@@ -131,7 +135,7 @@ def tile_expert_kernel(tc, x, weight1, weight2_words, weight2_scales, out):
             nc.scalar.copy(out=sorted_view[:, VECTOR_Q:], in_=rows[:, VECTOR_Q:])
 
         def quantise_w1(e, i):
-            c, half = units[i]
+            c, half = units(e)[i]
             if i == 0:
                 w1_codes[e] = w1_work.tile([P, PASSES, HALVES, F], U32, name="w1_codes", align_bytes=64)
                 w1_planes[e] = w1_work.tile([P, PASSES, HALVES, F], U8, name="w1_planes", align_bytes=64)
@@ -189,15 +193,12 @@ def tile_expert_kernel(tc, x, weight1, weight2_words, weight2_scales, out):
                 in_=g_grouped[e][:, s].rearrange("p k t -> p (k t)"),
             )
 
-        def second_matmul(e, s, odd_bank_copy):
-            if s == 0:
-                result[e] = out_pool.tile([P, TOKEN_TILES, H], F32, name="result")
+        def second_matmul(e, s):
             tokens = slice(s * P, (s + 1) * P)
-            out_rows = out[e].rearrange("(p s) n -> p s n", s=TOKEN_TILES)
             for n in range(OUT_TILES):
-                o_ps = bo_banks.tile([P, N_TILE], F32, name="o_ps", tag="bo")
+                out_bank[e, s, n] = bo_banks.tile([P, N_TILE], F32, name="o_ps", tag="bo")
                 nc.tensor.matmul_mx(
-                    out=o_ps[:],
+                    out=out_bank[e, s, n][:],
                     lhsT=g_codes[e][:, tokens].bitcast(FP8X4),
                     lhsT_scale=g_planes[e][:, tokens],
                     rhs=w2_bytes[e][:, n * PACK * N_TILE : (n + 1) * PACK * N_TILE].bitcast(FP8X4),
@@ -205,10 +206,14 @@ def tile_expert_kernel(tc, x, weight1, weight2_words, weight2_scales, out):
                     start=True,
                     stop=True,
                 )
-                copy = odd_bank_copy if n % 2 else nc.scalar.copy
-                columns = slice(n * N_TILE, (n + 1) * N_TILE)
-                copy(out=result[e][:, s, columns], in_=o_ps[:])
-                nc.sync.dma_start(out=out_rows[:, s, columns], in_=result[e][:, s, columns])
+
+        def store_bank(e, s, n, copy):
+            if s == 0 and n == 0:
+                result[e] = out_pool.tile([P, TOKEN_TILES, H], F32, name="result")
+            out_rows = out[e].rearrange("(p s) n -> p s n", s=TOKEN_TILES)
+            columns = slice(n * N_TILE, (n + 1) * N_TILE)
+            copy(out=result[e][:, s, columns], in_=out_bank[e, s, n][:])
+            nc.sync.dma_start(out=out_rows[:, s, columns], in_=result[e][:, s, columns])
 
         regroup_w1(0, 0)
         regroup_w1(0, 1)
@@ -221,40 +226,64 @@ def tile_expert_kernel(tc, x, weight1, weight2_words, weight2_scales, out):
         quantise_w1(0, 2)
         regroup_w1(0, 3)
         first_matmul(0, 0, a_banks, "a")
-        for e in range(1, E + 1):
-            this = e < E
-            last = e > 0
-            odd_bank_copy = nc.scalar.copy if this else nc.vector.tensor_copy
-            if this:
-                regroup_w1(e, 0)
-            if last:
-                quantise_w1(e - 1, 3)
-                first_matmul(e - 1, 1, bo_banks, "bo")
-                gelu(e - 1)
-            if this:
-                regroup_w1(e, 1)
-                quantise_w1(e, 0)
-            if last:
-                gate(e - 1, 0)
-            if this:
-                transpose_x(e)
-                regroup_w1(e, 2)
-            if last:
-                quantise_g(e - 1, 0)
-                gate(e - 1, 1)
-            if this:
-                quantise_w1(e, 1)
-            if last:
-                quantise_g(e - 1, 1)
-            if this:
-                regroup_x(e)
-                quantise_w1(e, 2)
-                quantise_x(e)
-            if last:
-                second_matmul(e - 1, 0, odd_bank_copy)
-            if this:
-                regroup_w1(e, 3)
-            if last:
-                second_matmul(e - 1, 1, odd_bank_copy)
-            if this:
-                first_matmul(e, 0, a_banks, "a")
+        on_scalar, on_vector = nc.scalar.copy, nc.vector.tensor_copy
+        for e in range(1, E - 1):
+            regroup_w1(e, 0)
+            quantise_w1(e - 1, 3)
+            first_matmul(e - 1, 1, bo_banks, "bo")
+            gelu(e - 1)
+            regroup_w1(e, 1)
+            quantise_w1(e, 0)
+            gate(e - 1, 0)
+            transpose_x(e)
+            regroup_w1(e, 2)
+            quantise_g(e - 1, 0)
+            gate(e - 1, 1)
+            quantise_w1(e, 1)
+            quantise_g(e - 1, 1)
+            regroup_x(e)
+            quantise_w1(e, 2)
+            quantise_x(e)
+            second_matmul(e - 1, 0)
+            store_bank(e - 1, 0, 0, on_scalar)
+            store_bank(e - 1, 0, 1, on_scalar)
+            regroup_w1(e, 3)
+            second_matmul(e - 1, 1)
+            store_bank(e - 1, 1, 0, on_scalar)
+            store_bank(e - 1, 1, 1, on_scalar)
+            first_matmul(e, 0, a_banks, "a")
+        e = E - 1
+        regroup_w1(e, 0)
+        quantise_w1(e - 1, 3)
+        first_matmul(e - 1, 1, bo_banks, "bo")
+        gelu(e - 1)
+        regroup_w1(e, 1)
+        quantise_w1(e, 0)
+        gate(e - 1, 0)
+        transpose_x(e)
+        regroup_x(e)
+        regroup_w1(e, 2)
+        quantise_g(e - 1, 0)
+        gate(e - 1, 1)
+        quantise_w1(e, 1)
+        quantise_g(e - 1, 1)
+        second_matmul(e - 1, 0)
+        second_matmul(e - 1, 1)
+        quantise_x(e)
+        first_matmul(e, 0, a_banks, "a")
+        regroup_w1(e, 3)
+        quantise_w1(e, 2)
+        store_bank(e - 1, 0, 0, on_scalar)
+        store_bank(e - 1, 0, 1, on_scalar)
+        gelu(e)
+        quantise_w1(e, 3)
+        first_matmul(e, 1, bo_banks, "bo")
+        store_bank(e - 1, 1, 0, on_scalar)
+        store_bank(e - 1, 1, 1, on_vector)
+        for s in range(TOKEN_TILES):
+            gate(e, s)
+            quantise_g(e, s)
+        for s in range(TOKEN_TILES):
+            second_matmul(e, s)
+            store_bank(e, s, 0, on_scalar)
+            store_bank(e, s, 1, on_vector)

@@ -79,8 +79,11 @@ def tile_expert_kernel(tc, x, weight1, weight2_words, weight2_scales, out):
 
         for e in range(E):
             load_w1(e, 0)
-            load_x(e)
+            if e < E - 1:
+                load_x(e)
             load_w1(e, 1)
+            if e == E - 1:
+                load_x(e)
             if e == 1:
                 for quadrant in range(4):
                     nc.sync.dma_start(

@@ -135,7 +135,9 @@ def tile_expert_kernel(tc, x, weight1, weight2_words, weight2_scales, out):
             w1_grouped[e, i] = w1_group.tile([P, F, PACK], BF16, name="w1_grouped", align_bytes=64)
             sorted_view = w1_grouped[e, i][:].rearrange("p (j q) t -> p q t j", j=PACK)
             nc.vector.tensor_copy(out=sorted_view[:, :VECTOR_Q], in_=rows[:, :VECTOR_Q])
-            nc.scalar.copy(out=sorted_view[:, VECTOR_Q:], in_=rows[:, VECTOR_Q:])
+            pairs_out = w1_grouped[e, i][:].rearrange("p (j q) (t u) -> p q t j u", j=PACK, u=2)
+            pairs_in = rows.rearrange("p q (t u) j -> p q t j u", u=2)
+            nc.scalar.copy(out=pairs_out[:, VECTOR_Q:], in_=pairs_in[:, VECTOR_Q:])
 
         def quantise_w1(e, i):
             c, half = units(e)[i]

@@ -133,8 +133,9 @@ def tile_expert_kernel(tc, x, weight1, weight2_words, weight2_scales, out):
             c, half = units(e)[i]
             rows = w1_rows[e, c, half]
             w1_grouped[e, i] = w1_group.tile([P, F, PACK], BF16, name="w1_grouped", align_bytes=64)
-            sorted_view = w1_grouped[e, i][:].rearrange("p (j q) t -> p q t j", j=PACK)
-            nc.vector.tensor_copy(out=sorted_view[:, :VECTOR_Q], in_=rows[:, :VECTOR_Q])
+            runs_out = w1_grouped[e, i][:].rearrange("p (j q v) t -> p q t v j", j=PACK, v=2)
+            runs_in = rows.rearrange("p (q v) t j -> p q t v j", v=2)
+            nc.vector.tensor_copy(out=runs_out[:, : VECTOR_Q // 2], in_=runs_in[:, : VECTOR_Q // 2])
             pairs_out = w1_grouped[e, i][:].rearrange("p (j q) (t u) -> p q t j u", j=PACK, u=2)
             pairs_in = rows.rearrange("p q (t u) j -> p q t j u", u=2)
             nc.scalar.copy(out=pairs_out[:, VECTOR_Q:], in_=pairs_in[:, VECTOR_Q:])
@@ -212,13 +213,13 @@ def tile_expert_kernel(tc, x, weight1, weight2_words, weight2_scales, out):
                     stop=True,
                 )
 
-        def store_bank(e, s, n, copy):
+        def store_bank(e, s, n, copy, queue=nc.sync):
             if s == 0 and n == 0:
                 result[e] = out_pool.tile([P, TOKEN_TILES, H], F32, name="result")
             out_rows = out[e].rearrange("(p s) n -> p s n", s=TOKEN_TILES)
             columns = slice(n * N_TILE, (n + 1) * N_TILE)
             copy(out=result[e][:, s, columns], in_=out_bank[e, s, n][:])
-            nc.sync.dma_start(out=out_rows[:, s, columns], in_=result[e][:, s, columns])
+            queue.dma_start(out=out_rows[:, s, columns], in_=result[e][:, s, columns])
 
         regroup_w1(0, 0)
         regroup_w1(0, 1)
@@ -290,5 +291,5 @@ def tile_expert_kernel(tc, x, weight1, weight2_words, weight2_scales, out):
             quantise_g(e, s)
         for s in range(TOKEN_TILES):
             second_matmul(e, s)
-            store_bank(e, s, 0, on_scalar)
+            store_bank(e, s, 0, on_scalar, nc.scalar)
             store_bank(e, s, 1, on_vector)

@@ -145,11 +145,14 @@ def tile_expert_kernel(tc, x, weight1, weight2_words, weight2_scales, out):
             if i == 0:
                 w1_codes[e] = w1_work.tile([P, PASSES, HALVES, F], U32, name="w1_codes", align_bytes=64)
                 w1_planes[e] = w1_work.tile([P, PASSES, HALVES, F], U8, name="w1_planes", align_bytes=64)
-            nc.vector.quantize_mx(
-                out=w1_codes[e][:, c, half, :].bitcast(FP8X4),
-                scales=w1_planes[e][:, c, half, :],
-                in_=w1_grouped[e, i][:].rearrange("p n t -> p (n t)"),
-            )
+            pieces = 2 if (e, i) == (E - 1, 3) else 1
+            for k in range(pieces):
+                columns = slice(k * F // pieces, (k + 1) * F // pieces)
+                nc.vector.quantize_mx(
+                    out=w1_codes[e][:, c, half, columns].bitcast(FP8X4),
+                    scales=w1_planes[e][:, c, half, columns],
+                    in_=w1_grouped[e, i][:, columns].rearrange("p n t -> p (n t)"),
+                )
 
         def first_matmul(e, half, banks, tag):
             for s in range(TOKEN_TILES):
@@ -219,7 +222,11 @@ def tile_expert_kernel(tc, x, weight1, weight2_words, weight2_scales, out):
             out_rows = out[e].rearrange("(p s) n -> p s n", s=TOKEN_TILES)
             columns = slice(n * N_TILE, (n + 1) * N_TILE)
             copy(out=result[e][:, s, columns], in_=out_bank[e, s, n][:])
-            queue.dma_start(out=out_rows[:, s, columns], in_=result[e][:, s, columns])
+            if e < E - 2:
+                if s == TOKEN_TILES - 1 and n == OUT_TILES - 1:
+                    queue.dma_start(out=out_rows, in_=result[e][:])
+            else:
+                queue.dma_start(out=out_rows[:, s, columns], in_=result[e][:, s, columns])
 
         regroup_w1(0, 0)
         regroup_w1(0, 1)
@@ -285,7 +292,7 @@ def tile_expert_kernel(tc, x, weight1, weight2_words, weight2_scales, out):
         quantise_w1(e, 3)
         first_matmul(e, 1, bo_banks, "bo")
         store_bank(e - 1, 1, 0, on_scalar)
-        store_bank(e - 1, 1, 1, on_vector)
+        store_bank(e - 1, 1, 1, on_scalar)
         for s in range(TOKEN_TILES):
             gate(e, s)
             quantise_g(e, s)

from contextlib import ExitStack

import concourse.mybir as mybir
from concourse.masks import make_identity

E, T, H, F = 4, 256, 1024, 512
FLOPS = 2 * E * T * H * (2 * F) + 2 * E * T * F * H

BF16 = mybir.dt.bfloat16
F32 = mybir.dt.float32
I32 = mybir.dt.int32
U32 = mybir.dt.uint32
U8 = mybir.dt.uint8
FP8X4 = mybir.dt.float8_e4m3fn_x4

P = 128
PACK = 4
K_PASS = P * PACK
PASSES = H // K_PASS
TOKEN_TILES = T // P
HALVES = 2
N_TILE = 512
OUT_TILES = H // N_TILE

VECTOR_Q = 80


def tile_expert_kernel(tc, x, weight1, weight2_words, weight2_scales, out):
    nc = tc.nc
    with ExitStack() as stack:
        pool = lambda name, bufs: stack.enter_context(tc.tile_pool(name=name, bufs=bufs))
        bank = lambda name, bufs: stack.enter_context(tc.psum_pool(name=name, bufs=bufs))
        consts = pool("consts", 1)
        x_pool = pool("x_pool", E)
        w1_pool = pool("w1_pool", E * PASSES)
        w2_pool = pool("w2_pool", E)
        out_pool = pool("out_pool", E)
        x_work = pool("x_work", 2)
        w1_group = pool("w1_group", 3)
        w1_work = pool("w1_work", 2)
        g_work = pool("g_work", 2)
        xt_banks = bank("xt_banks", PASSES)
        a_banks = bank("a_banks", TOKEN_TILES)
        bo_banks = bank("bo_banks", 4)
        stack.enter_context(tc.manual_schedule())

        w2_planes = consts.tile([P, H], U8, align_bytes=64)
        nc.vector.memset(w2_planes[:].bitcast(I32), 0)
        identity = consts.tile([P, P], F32)
        make_identity(nc, identity[:])
        table_warmer = consts.tile([P, 1], F32)
        nc.scalar.activation(
            out=table_warmer[:],
            in_=identity[:, 0:1],
            func=mybir.ActivationFunctionType.Gelu_apprx_tanh,
        )

        x_rows, w1_rows, w2_bytes = {}, {}, {}

        def load_x(e):
            x_rows[e] = x_pool.tile([P, TOKEN_TILES, H], BF16, name="x_rows")
            nc.sync.dma_start(out=x_rows[e][:], in_=x[e].rearrange("(p s) k -> p s k", s=TOKEN_TILES))

        def load_w1(e, c):
            first = (e * PASSES + c) * P
            tile_rows = w1_pool.tile([P, PACK * 2 * F], BF16, name="w1_rows")
            nc.sync.dma_start(out=tile_rows[:], in_=weight1[first : first + P, :])
            view = tile_rows[:].rearrange("p (t half q j) -> p half q t j", t=PACK, half=HALVES, j=PACK)
            for half in range(HALVES):
                w1_rows[e, c, half] = view[:, half]


        def load_w2(e):
            w2_bytes[e] = w2_pool.tile([P, PACK * H], U8, name="w2_bytes", align_bytes=64)
            nc.sync.dma_start(
                out=w2_bytes[e][:].bitcast(I32),
                in_=weight2_words[e].rearrange("p n t -> p (n t)").bitcast(I32),
            )

        for e in range(E):
            load_w1(e, 0)
            if e < E - 1:
                load_x(e)
            load_w1(e, 1)
            if e == E - 1:
                load_x(e)
            if e == 1:
                for quadrant in range(4):
                    nc.sync.dma_start(
                        out=w2_planes[32 * quadrant : 32 * quadrant + 4 * E, :].bitcast(I32),
                        in_=weight2_scales[:, 4 * quadrant : 4 * quadrant + 4, :].bitcast(I32),
                    )
            if e > 0:
                load_w2(e - 1)
        load_w2(E - 1)

        def units(e):
            if e < E - 1:
                return [(c, half) for c in range(PASSES) for half in range(HALVES)]
            return [(c, half) for half in range(HALVES) for c in range(PASSES)]

        x_bank, x_grouped, x_codes, x_planes = {}, {}, {}, {}
        w1_grouped, w1_codes, w1_planes = {}, {}, {}
        h_t, activated, g_grouped, g_codes, g_planes, out_bank, result = {}, {}, {}, {}, {}, {}, {}

        def transpose_x(e):
            for c in range(PASSES):
                x_bank[e, c] = xt_banks.tile([P, 2, T], F32, name="x_bank")
                for s in range(TOKEN_TILES):
                    words = x_rows[e][:, s, c * K_PASS : (c + 1) * K_PASS].bitcast(F32)
                    for u in range(2):
                        nc.tensor.transpose(
                            x_bank[e, c][:, u, s * P : (s + 1) * P], words[:, u::2], identity[:]
                        )

        def regroup_x(e):
            x_grouped[e] = x_work.tile([P, PASSES, T, PACK], BF16, name="x_grouped", align_bytes=64)
            for c in range(PASSES):
                nc.scalar.copy(
                    out=x_grouped[e][:, c].bitcast(F32), in_=x_bank[e, c][:].rearrange("p u k -> p k u")
                )

        def quantise_x(e):
            x_codes[e] = x_work.tile([P, PASSES, T], U32, name="x_codes", align_bytes=64)
            x_planes[e] = x_work.tile([P, PASSES, T], U8, name="x_planes", align_bytes=64)
            nc.vector.quantize_mx(
                out=x_codes[e][:].rearrange("p c k -> p (c k)").bitcast(FP8X4),
                scales=x_planes[e][:].rearrange("p c k -> p (c k)"),
                in_=x_grouped[e][:].rearrange("p c k t -> p (c k t)"),
            )

        def regroup_w1(e, i):
            c, half = units(e)[i]
            rows = w1_rows[e, c, half]
            w1_grouped[e, i] = w1_group.tile([P, F, PACK], BF16, name="w1_grouped", align_bytes=64)
            runs_out = w1_grouped[e, i][:].rearrange("p (j q v) t -> p q t v j", j=PACK, v=2)
            runs_in = rows.rearrange("p (q v) t j -> p q t v j", v=2)
            nc.vector.tensor_copy(out=runs_out[:, : VECTOR_Q // 2], in_=runs_in[:, : VECTOR_Q // 2])
            pairs_out = w1_grouped[e, i][:].rearrange("p (j q) (t u) -> p q t j u", j=PACK, u=2)
            pairs_in = rows.rearrange("p q (t u) j -> p q t j u", u=2)
            nc.scalar.copy(out=pairs_out[:, VECTOR_Q:], in_=pairs_in[:, VECTOR_Q:])

        def quantise_w1(e, i):
            c, half = units(e)[i]
            if i == 0:
                w1_codes[e] = w1_work.tile([P, PASSES, HALVES, F], U32, name="w1_codes", align_bytes=64)
                w1_planes[e] = w1_work.tile([P, PASSES, HALVES, F], U8, name="w1_planes", align_bytes=64)
            pieces = 2 if (e, i) == (E - 1, 3) else 1
            for k in range(pieces):
                columns = slice(k * F // pieces, (k + 1) * F // pieces)
                nc.vector.quantize_mx(
                    out=w1_codes[e][:, c, half, columns].bitcast(FP8X4),
                    scales=w1_planes[e][:, c, half, columns],
                    in_=w1_grouped[e, i][:, columns].rearrange("p n t -> p (n t)"),
                )

        def first_matmul(e, half, banks, tag):
            for s in range(TOKEN_TILES):
                h_t[e, half, s] = banks.tile([P, PACK, P], F32, name="h_t", tag=tag)
                tokens = slice(s * P, (s + 1) * P)
                for j in range(PACK):
                    columns = slice(j * P, (j + 1) * P)
                    for c in range(PASSES):
                        nc.tensor.matmul_mx(
                            out=h_t[e, half, s][:, j, :],
                            lhsT=w1_codes[e][:, c, half, columns].bitcast(FP8X4),
                            lhsT_scale=w1_planes[e][:, c, half, columns],
                            rhs=x_codes[e][:, c, tokens].bitcast(FP8X4),
                            rhs_scale=x_planes[e][:, c, tokens],
                            start=(c == 0),
                            stop=(c == PASSES - 1),
                        )

        def gelu(e):
            for s in range(TOKEN_TILES):
                activated[e, s] = g_work.tile([P, P, PACK], F32, name="activated")
                nc.scalar.activation(
                    out=activated[e, s][:],
                    in_=h_t[e, 0, s][:].rearrange("p j k -> p k j"),
                    func=mybir.ActivationFunctionType.Gelu_apprx_tanh,
                )

        def gate(e, s):
            if s == 0:
                g_grouped[e] = g_work.tile(
                    [P, TOKEN_TILES, P, PACK], BF16, name="g_grouped", align_bytes=64
                )
            nc.vector.tensor_mul(
                out=g_grouped[e][:, s],
                in0=activated[e, s][:],
                in1=h_t[e, 1, s][:].rearrange("p j k -> p k j"),
            )

        def quantise_g(e, s):
            if s == 0:
                g_codes[e] = g_work.tile([P, T], U32, name="g_codes", align_bytes=64)
                g_planes[e] = g_work.tile([P, T], U8, name="g_planes", align_bytes=64)
            tokens = slice(s * P, (s + 1) * P)
            nc.vector.quantize_mx(
                out=g_codes[e][:, tokens].bitcast(FP8X4),
                scales=g_planes[e][:, tokens],
                in_=g_grouped[e][:, s].rearrange("p k t -> p (k t)"),
            )

        def second_matmul(e, s):
            tokens = slice(s * P, (s + 1) * P)
            for n in range(OUT_TILES):
                out_bank[e, s, n] = bo_banks.tile([P, N_TILE], F32, name="o_ps", tag="bo")
                nc.tensor.matmul_mx(
                    out=out_bank[e, s, n][:],
                    lhsT=g_codes[e][:, tokens].bitcast(FP8X4),
                    lhsT_scale=g_planes[e][:, tokens],
                    rhs=w2_bytes[e][:, n * PACK * N_TILE : (n + 1) * PACK * N_TILE].bitcast(FP8X4),
                    rhs_scale=w2_planes[4 * e : P, n * N_TILE : (n + 1) * N_TILE],
                    start=True,
                    stop=True,
                )

        def store_bank(e, s, n, copy, queue=nc.sync):
            if s == 0 and n == 0:
                result[e] = out_pool.tile([P, TOKEN_TILES, H], F32, name="result")
            out_rows = out[e].rearrange("(p s) n -> p s n", s=TOKEN_TILES)
            columns = slice(n * N_TILE, (n + 1) * N_TILE)
            copy(out=result[e][:, s, columns], in_=out_bank[e, s, n][:])
            if e < E - 2:
                if s == TOKEN_TILES - 1 and n == OUT_TILES - 1:
                    queue.dma_start(out=out_rows, in_=result[e][:])
            else:
                queue.dma_start(out=out_rows[:, s, columns], in_=result[e][:, s, columns])

        regroup_w1(0, 0)
        regroup_w1(0, 1)
        quantise_w1(0, 0)
        transpose_x(0)
        quantise_w1(0, 1)
        regroup_x(0)
        regroup_w1(0, 2)
        quantise_x(0)
        quantise_w1(0, 2)
        regroup_w1(0, 3)
        first_matmul(0, 0, a_banks, "a")
        on_scalar, on_vector = nc.scalar.copy, nc.vector.tensor_copy
        for e in range(1, E - 1):
            regroup_w1(e, 0)
            quantise_w1(e - 1, 3)
            first_matmul(e - 1, 1, bo_banks, "bo")
            gelu(e - 1)
            regroup_w1(e, 1)
            quantise_w1(e, 0)
            gate(e - 1, 0)
            transpose_x(e)
            regroup_w1(e, 2)
            quantise_g(e - 1, 0)
            gate(e - 1, 1)
            quantise_w1(e, 1)
            quantise_g(e - 1, 1)
            regroup_x(e)
            quantise_w1(e, 2)
            quantise_x(e)
            second_matmul(e - 1, 0)
            store_bank(e - 1, 0, 0, on_scalar)
            store_bank(e - 1, 0, 1, on_scalar)
            regroup_w1(e, 3)
            second_matmul(e - 1, 1)
            store_bank(e - 1, 1, 0, on_scalar)
            store_bank(e - 1, 1, 1, on_scalar)
            first_matmul(e, 0, a_banks, "a")
        e = E - 1
        regroup_w1(e, 0)
        quantise_w1(e - 1, 3)
        first_matmul(e - 1, 1, bo_banks, "bo")
        gelu(e - 1)
        regroup_w1(e, 1)
        quantise_w1(e, 0)
        gate(e - 1, 0)
        transpose_x(e)
        regroup_x(e)
        regroup_w1(e, 2)
        quantise_g(e - 1, 0)
        gate(e - 1, 1)
        quantise_w1(e, 1)
        quantise_g(e - 1, 1)
        second_matmul(e - 1, 0)
        second_matmul(e - 1, 1)
        quantise_x(e)
        first_matmul(e, 0, a_banks, "a")
        regroup_w1(e, 3)
        quantise_w1(e, 2)
        store_bank(e - 1, 0, 0, on_scalar)
        store_bank(e - 1, 0, 1, on_scalar)
        gelu(e)
        quantise_w1(e, 3)
        first_matmul(e, 1, bo_banks, "bo")
        store_bank(e - 1, 1, 0, on_scalar)
        store_bank(e - 1, 1, 1, on_scalar)
        for s in range(TOKEN_TILES):
            gate(e, s)
            quantise_g(e, s)
        for s in range(TOKEN_TILES):
            second_matmul(e, s)
            store_bank(e, s, 0, on_scalar, nc.scalar)
            store_bank(e, s, 1, on_vector)
